import numpy as np
import ml_dtypes


def mxq(x, axis, fmt="e4m3"):
    dtype, down = {"e4m3": (ml_dtypes.float8_e4m3fn, 7), "e5m2": (ml_dtypes.float8_e5m2, 14)}[fmt]
    v = np.moveaxis(np.asarray(x, np.float32).astype(ml_dtypes.bfloat16).astype(np.float64), axis, -1)
    blocks = v.reshape(v.shape[:-1] + (-1, 32))
    amax = np.abs(blocks).max(-1, keepdims=True)
    byte = np.maximum(np.where(amax > 0, np.frexp(amax)[1] - 1 + 127, 0) - down, 1)
    scale = np.exp2(byte - 127.0)
    codes = (blocks / scale).astype(np.float32).astype(dtype).astype(np.float64)
    return np.moveaxis((codes * scale).reshape(v.shape), -1, axis)


WIDE = False


def mx_kscale(k):
    if not WIDE:
        return np.ones(k)
    levels = np.array([10, -10, 5, -5, 0])
    if k % 512:
        return np.exp2(np.random.permutation(np.resize(levels, k // 32))).repeat(32)
    a = np.empty((k // 512, 16))
    for p in range(k // 512):
        a[p, :8] = np.random.permutation(np.resize(levels, 8))
        for g in range(8):
            far = levels[np.abs(levels - a[p, g]) >= 10]
            a[p, g + 8] = far[np.random.randint(len(far))]
    return np.exp2(a.ravel()).repeat(32)


BF16 = ml_dtypes.bfloat16


def bf(x):
    return np.asarray(x, np.float32).astype(BF16)


def f64(x):
    return np.asarray(x).astype(np.float64)


B, S, D, H, NOPE, ROPE, VD, KV_RANK, Q_RANK = 4, 2048, 1024, 2, 64, 64, 128, 512, 512
EPS = 1e-6
THETA = 10000.0
LAT = 0.005
HALF = ROPE // 2
QK = NOPE + ROPE


def rmsnorm(v, g):
    return v * (1.0 / np.sqrt(np.mean(v * v, axis=-1, keepdims=True) + EPS)) * g


def rope(v):
    inv = 1.0 / THETA ** (np.arange(HALF) / HALF)
    ang = np.arange(S)[:, None] * inv[None, :]
    cos = np.cos(ang)[None, :, None, :]
    sin = np.sin(ang)[None, :, None, :]
    v1, v2 = v[..., :HALF], v[..., HALF:]
    return np.concatenate([v1 * cos - v2 * sin, v2 * cos + v1 * sin], axis=-1)


def setup_inputs():
    s, t = mx_kscale(D), mx_kscale(Q_RANK)
    return {"x": bf(np.random.standard_normal((B, S, D)) * s),
            "w_dq": bf(np.random.standard_normal((D, Q_RANK)) * LAT / np.sqrt(D) / s[:, None]),
            "q_a_norm": bf((1.0 + 0.1 * np.random.standard_normal(Q_RANK)) * t),
            "w_uq": bf(np.random.standard_normal((Q_RANK, H * QK)) / np.sqrt(Q_RANK) / t[:, None])}


def reference(x, w_dq, q_a_norm, w_uq):
    c_q = mxq(f64(x), 2, "e4m3") @ mxq(f64(w_dq), 0, "e4m3")
    h = rmsnorm(c_q, f64(q_a_norm))
    q = (mxq(h, 2, "e4m3") @ mxq(f64(w_uq), 0, "e4m3")).reshape(B, S, H, QK)
    q_nope, q_pe = q[..., :NOPE], q[..., NOPE:]
    return np.concatenate([q_nope, rope(q_pe)], axis=-1)

@@ -1,0 +1,289 @@
+from contextlib import ExitStack
+import math
+
+import concourse.mybir as mybir
+from concourse.masks import make_identity
+
+F32 = mybir.dt.float32
+BF16 = mybir.dt.bfloat16
+I32 = mybir.dt.int32
+U32 = mybir.dt.uint32
+U8 = mybir.dt.uint8
+FP8X4 = mybir.dt.float8_e4m3fn_x4
+ALU = mybir.AluOpType
+ACT = mybir.ActivationFunctionType
+
+P = 128
+B, S, D, H, NOPE, ROPE, Q_RANK = 4, 2048, 1024, 2, 64, 64, 512
+QK = NOPE + ROPE
+HALF = ROPE // 2
+NOUT = H * QK
+EPS = 1e-6
+THETA = 10000.0
+TPB = S // P
+UNIT = 2
+UPB = TPB // UNIT
+UNITS = B * UPB
+AHEAD = 6
+MANUAL = True
+VEC_MOD = 2
+VEC_COPY = ()
+LAG_M1, LAG_NORM, LAG_TH, LAG_CH, LAG_QH, LAG_M2, LAG_ROPE = 3, 4, 5, 5, 5, 6, 7
+
+FLOPS = 2 * B * S * (D * Q_RANK + Q_RANK * NOUT)
+
+GRID = 2 ** 15
+
+
+def tile_multiheadlatentattention_pa_t_kernel(tc, x, w_dq, q_a_norm, w_uq, out):
+    nc = tc.nc
+    xv = x.rearrange("b (p t) k -> b p t k", t=TPB)
+    ov = out.rearrange("b (p t) h f -> b p t (h f)", t=TPB)
+
+    with ExitStack() as ctx:
+        const = ctx.enter_context(tc.tile_pool(name="const", bufs=1))
+        setup = ctx.enter_context(tc.tile_pool(name="setup", bufs=1))
+        xpool = ctx.enter_context(tc.tile_pool(name="xpool", bufs=AHEAD + 1))
+        work = ctx.enter_context(tc.tile_pool(name="work", bufs=3))
+        small = ctx.enter_context(tc.tile_pool(name="small", bufs=4))
+        psum = ctx.enter_context(tc.psum_pool(name="psum", bufs=1))
+        if MANUAL:
+            ctx.enter_context(tc.manual_schedule())
+
+        st = {}
+
+        def load(u):
+            x_sb = xpool.tile([P, UNIT, D], BF16, name="x_sb")
+            b, t0 = u // UPB, (u % UPB) * UNIT
+            nc.sync.dma_start(out=x_sb[:], in_=xv[b, :, t0:t0 + UNIT, :])
+            st["x", u] = x_sb
+
+        w_raw = setup.tile([P, 2, 4 * Q_RANK], BF16)
+        w_view = w_dq.rearrange("(g p t) c -> p g (t c)", g=2, p=P, t=4)
+        nc.sync.dma_start(out=w_raw[:, 0, :], in_=w_view[:, 0, :])
+        nc.sync.dma_start(out=w_raw[:, 1, :], in_=w_view[:, 1, :])
+        for u in range(AHEAD):
+            load(u)
+        u_raw = setup.tile([P, 4, NOUT], BF16)
+        nc.scalar.dma_start(out=u_raw[:], in_=w_uq.rearrange("(p j) n -> p j n", j=4))
+
+        pos_i = setup.tile([P, TPB], I32)
+        nc.gpsimd.iota(pos_i[:], pattern=[[1, TPB]], base=0, channel_multiplier=TPB)
+        ident_f = const.tile([P, P], F32)
+        make_identity(nc, ident_f[:])
+        g_b = const.tile([P, Q_RANK], BF16)
+        g_raw = setup.tile([P, Q_RANK], BF16)
+        nc.gpsimd.dma_start(out=g_raw[:], in_=q_a_norm.partition_broadcast(P))
+        nc.gpsimd.tensor_copy(out=g_b[:].rearrange("p (j m) -> p j m", j=4),
+                              in_=g_raw[:].rearrange("p (m j) -> p j m", j=4))
+        ident_b = const.tile([P, P], BF16)
+        make_identity(nc, ident_b[:])
+        neg_half = const.tile([P, UNIT], F32)
+        nc.gpsimd.memset(neg_half[:], -0.5)
+
+        zero = setup.tile([P, 1], F32)
+        nc.vector.memset(zero[:], 0.0)
+        warm = setup.tile([P, 1], F32)
+        nc.scalar.activation(out=warm[:], in_=zero[:], func=ACT.Sin)
+        pos_f = setup.tile([P, TPB], F32)
+        nc.vector.tensor_copy(out=pos_f[:], in_=pos_i[:])
+        turn_i = setup.tile([P, 2, HALF, TPB], I32)
+        turn_lo = setup.tile([P, HALF, TPB], F32)
+        for i in range(HALF):
+            freq = 1.0 / THETA ** (i / HALF) / (2.0 * math.pi)
+            f_hi = math.floor(freq * GRID)
+            f_lo = freq - f_hi / GRID
+            nc.vector.tensor_scalar(out=turn_i[:, 0, i, :], in0=pos_f[:], scalar1=float(f_hi),
+                                    scalar2=float(GRID // 2), op0=ALU.mult, op1=ALU.add)
+            nc.scalar.activation(out=turn_lo[:, i, :], in_=pos_f[:], func=ACT.Copy, scale=f_lo)
+        nc.vector.tensor_scalar(out=turn_i[:, 1], in0=turn_i[:, 0], scalar1=float(GRID // 4),
+                                scalar2=None, op0=ALU.add)
+        nc.vector.tensor_scalar(out=turn_i[:], in0=turn_i[:], scalar1=GRID - 1,
+                                scalar2=None, op0=ALU.bitwise_and)
+        frac = setup.tile([P, 2, TPB * HALF], F32)
+        negf = setup.tile([P, 2, HALF, TPB], F32)
+        cos_t = const.tile([P, TPB, HALF], F32)
+        sin_t = const.tile([P, TPB, 2, HALF], F32)
+
+        def tables_vector():
+            nc.vector.scalar_tensor_tensor(
+                out=frac[:], in0=turn_i[:].rearrange("p a i t -> p a (i t)"), scalar=1.0 / GRID,
+                in1=turn_lo[:].rearrange("p i t -> p (i t)").unsqueeze(1).to_broadcast([P, 2, TPB * HALF]),
+                op0=ALU.mult, op1=ALU.add)
+            nc.vector.scalar_tensor_tensor(
+                out=negf[:].rearrange("p a i t -> p a (i t)"), in0=frac[:], scalar=1.0, in1=frac[:],
+                op0=ALU.is_ge, op1=ALU.subtract)
+
+        def tables_scalar():
+            by_pos = negf[:].rearrange("p a i t -> p a t i")
+            nc.scalar.activation(out=cos_t[:], in_=by_pos[:, 1], func=ACT.Sin, scale=-2.0 * math.pi, bias=-math.pi)
+            nc.scalar.activation(out=sin_t[:, :, 0, :], in_=by_pos[:, 0], func=ACT.Sin,
+                                 scale=-2.0 * math.pi, bias=-math.pi)
+
+        def tables_negate():
+            nc.gpsimd.tensor_scalar(out=sin_t[:, :, 1, :], in0=sin_t[:, :, 0, :], scalar1=-1.0, scalar2=0.0,
+                                    op0=ALU.mult, op1=ALU.add)
+
+        wdq_c = const.tile([P, 2, Q_RANK], U32, align_bytes=64)
+        wdq_s = const.tile([P, 2, Q_RANK], U8, align_bytes=64)
+        w_grps = []
+        for g in range(2):
+            w_grp = setup.tile([P, Q_RANK, 4], BF16, align_bytes=64, name="w_grp%d" % g)
+            nc.vector.tensor_copy(out=w_grp[:].rearrange("p (j m) t -> p j m t", j=4),
+                                  in_=w_raw[:, g, :].rearrange("p (t m j) -> p j m t", t=4, j=4))
+            w_grps.append(w_grp)
+        for g in range(2):
+            nc.vector.quantize_mx(out=wdq_c[:, g, :].bitcast(FP8X4), scales=wdq_s[:, g, :],
+                                  in_=w_grps[g][:].rearrange("p c t -> p (c t)"))
+        wuq_c = const.tile([P, NOUT], U32, align_bytes=64)
+        wuq_s = const.tile([P, NOUT], U8, align_bytes=64)
+        u_grp = setup.tile([P, 2, H, NOPE, 4], BF16, align_bytes=64)
+
+        def weights_up():
+            u_src = u_raw[:].rearrange("p j (h r f) -> p r h f j", h=H, r=2)
+            for r in range(2):
+                nc.vector.tensor_copy(out=u_grp[:, r], in_=u_src[:, r])
+            nc.vector.quantize_mx(out=wuq_c[:].bitcast(FP8X4), scales=wuq_s[:],
+                                  in_=u_grp[:].rearrange("p r h f j -> p (r h f j)"))
+
+        def t_x(u, i):
+            if i == 0:
+                st["xg", u] = work.tile([P, UNIT, 2, P, 4], BF16, align_bytes=64, name="xg")
+            xt = psum.tile([P, 4, P], F32, name="xt", bufs=2)
+            words = st["x", u][:, i, :].bitcast(F32)
+            for a in range(4):
+                first = 2 * P * (a // 2) + a % 2
+                nc.tensor.transpose(xt[:, a, :], words[:, first:first + 2 * P - 1:2], ident_f[:])
+            st["xt", u, i] = xt
+
+        def c_x(u, i):
+            planes = st["xt", u, i][:].rearrange("p (g u) w -> p g w u", u=2)
+            dst = st["xg", u][:, i].bitcast(F32)
+            if i == 1 and u % VEC_MOD in VEC_COPY and u < UNITS - 1:
+                nc.vector.tensor_copy(out=dst, in_=planes)
+            else:
+                nc.scalar.copy(out=dst, in_=planes)
+
+        def q_x(u):
+            xc = work.tile([P, UNIT * 2 * P], U32, align_bytes=64, name="xc", bufs=5)
+            xs = work.tile([P, UNIT * 2 * P], U8, align_bytes=64, name="xs", bufs=5)
+            nc.vector.quantize_mx(out=xc[:].bitcast(FP8X4), scales=xs[:],
+                                  in_=st["xg", u][:].rearrange("p i g w t -> p (i g w t)"))
+            st["xc", u] = (xc, xs)
+
+        def mx1(u, i):
+            xc, xs = st["xc", u]
+            c_ps = psum.tile([P, Q_RANK], F32, name="c_ps", bufs=4)
+            for g in range(2):
+                cols = slice((2 * i + g) * P, (2 * i + g + 1) * P)
+                nc.tensor.matmul_mx(out=c_ps[:], lhsT=xc[:, cols].bitcast(FP8X4), lhsT_scale=xs[:, cols],
+                                    rhs=wdq_c[:, g, :].bitcast(FP8X4), rhs_scale=wdq_s[:, g, :],
+                                    start=(g == 0), stop=(g == 1))
+            st["c", u, i] = c_ps
+
+        def s_q(u, i):
+            if i == 0:
+                st["ss", u] = small.tile([P, UNIT], F32, name="ss")
+            junk = work.tile([P, Q_RANK], BF16, name="junk")
+            nc.scalar.activation(out=junk[:], in_=st["c", u, i][:], func=ACT.Square,
+                                 accum_out=st["ss", u][:, i:i + 1])
+
+        def r_t(u):
+            ms = small.tile([P, UNIT], F32, name="ms")
+            nc.gpsimd.tensor_scalar(out=ms[:], in0=st["ss", u][:], scalar1=1.0 / Q_RANK, scalar2=EPS,
+                                    op0=ALU.mult, op1=ALU.add)
+            rstd = small.tile([P, UNIT], F32, name="rstd")
+            nc.gpsimd.tensor_tensor(out=rstd[:], in0=ms[:], in1=neg_half[:], op=ALU.pow)
+            st["rstd", u] = rstd
+
+        def norm(u):
+            rstd = st["rstd", u]
+            h_sb = work.tile([P, UNIT, Q_RANK], BF16, name="h_sb")
+            for i in range(UNIT):
+                nc.vector.scalar_tensor_tensor(out=h_sb[:, i, :], in0=st["c", u, i][:], scalar=rstd[:, i:i + 1],
+                                               in1=g_b[:], op0=ALU.mult, op1=ALU.mult)
+            st["h", u] = h_sb
+
+        def t_h(u, i):
+            if i == 0:
+                st["ht", u] = psum.tile([P, UNIT, 4, P], BF16, name="ht", bufs=1)
+            for j in range(4):
+                nc.tensor.transpose(st["ht", u][:, i, j, :], st["h", u][:, i, j * P:(j + 1) * P], ident_b[:])
+
+        def c_h(u):
+            hg = work.tile([P, UNIT, P, 4], BF16, align_bytes=64, name="hg")
+            nc.scalar.copy(out=hg[:], in_=st["ht", u][:].rearrange("p i j w -> p i w j"))
+            st["hg", u] = hg
+
+        def q_h(u):
+            hc = work.tile([P, UNIT * P], U32, align_bytes=64, name="hc")
+            hs = work.tile([P, UNIT * P], U8, align_bytes=64, name="hs")
+            nc.vector.quantize_mx(out=hc[:].bitcast(FP8X4), scales=hs[:],
+                                  in_=st["hg", u][:].rearrange("p i w j -> p (i w j)"))
+            st["hc", u] = (hc, hs)
+
+        def mx2(u):
+            hc, hs = st["hc", u]
+            q_ps = psum.tile([P, UNIT, NOUT], F32, name="q_ps", bufs=1)
+            for i in range(UNIT):
+                cols = slice(i * P, (i + 1) * P)
+                nc.tensor.matmul_mx(out=q_ps[:, i, :], lhsT=hc[:, cols].bitcast(FP8X4), lhsT_scale=hs[:, cols],
+                                    rhs=wuq_c[:].bitcast(FP8X4), rhs_scale=wuq_s[:], start=True, stop=True)
+            st["q", u] = q_ps
+
+        def rope(u):
+            q_ps = st["q", u]
+            b, t0 = u // UPB, (u % UPB) * UNIT
+            o_sb = work.tile([P, UNIT, H, QK], F32, name="o_sb", bufs=4)
+            by_cos = work.tile([P, UNIT, H, 2, HALF], F32, name="by_cos")
+            by_sin = work.tile([P, UNIT, H, 2, HALF], F32, name="by_sin")
+            nc.vector.tensor_tensor(
+                out=by_cos[:].rearrange("p i h r f -> p i (h r) f"),
+                in0=q_ps[:, :, H * NOPE:].rearrange("p i (a f) -> p i a f", f=HALF),
+                in1=cos_t[:, t0:t0 + UNIT, :].unsqueeze(2).to_broadcast([P, UNIT, 2 * H, HALF]),
+                op=ALU.mult)
+            nc.vector.tensor_tensor(
+                out=by_sin[:].rearrange("p i h r f -> p i h (r f)"),
+                in0=q_ps[:, :, H * NOPE:].rearrange("p i (h f) -> p i h f", h=H),
+                in1=sin_t[:, t0:t0 + UNIT].rearrange("p i r f -> p i (r f)").unsqueeze(2).to_broadcast(
+                    [P, UNIT, H, ROPE]),
+                op=ALU.mult)
+            nc.vector.tensor_copy(out=o_sb[:, :, :, 0:NOPE],
+                                  in_=q_ps[:, :, 0:H * NOPE].rearrange("p i (h f) -> p i h f", h=H))
+            adder = nc.vector if u == UNITS - 1 else nc.gpsimd
+            for r in range(2):
+                adder.tensor_tensor(out=o_sb[:, :, :, NOPE + r * HALF:NOPE + (r + 1) * HALF],
+                                        in0=by_cos[:, :, :, r, :], in1=by_sin[:, :, :, 1 - r, :], op=ALU.add)
+            nc.sync.dma_start(out=ov[b, :, t0:t0 + UNIT, :], in_=o_sb[:].rearrange("p i h f -> p i (h f)"))
+
+        def on(fn, u, *half):
+            if 0 <= u < UNITS:
+                fn(u, *half)
+
+        for s in range(UNITS + LAG_ROPE):
+            on(rope, s - LAG_ROPE)
+            on(norm, s - LAG_NORM)
+            on(mx1, s - LAG_M1, 0)
+            on(s_q, s - LAG_M1, 0)
+            on(t_x, s, 0)
+            on(c_x, s, 0)
+            on(t_h, s - LAG_TH, 0)
+            on(t_h, s - LAG_TH, 1)
+            on(c_h, s - LAG_CH)
+            on(mx1, s - LAG_M1, 1)
+            on(s_q, s - LAG_M1, 1)
+            if s == LAG_M1:
+                tables_scalar()
+            on(r_t, s - LAG_M1)
+            if s == LAG_M1:
+                tables_negate()
+            on(t_x, s, 1)
+            on(mx2, s - LAG_M2)
+            on(c_x, s, 1)
+            on(q_x, s - 1)
+            if s == 1:
+                tables_vector()
+            if s == 2:
+                weights_up()
+            on(q_h, s - LAG_QH)
+            on(load, s + AHEAD)

@@ -74,10 +74,8 @@ def tile_multiheadlatentattention_pa_t_kernel(tc, x, w_dq, q_a_norm, w_uq, out):
         g_b = const.tile([P, Q_RANK], BF16)
         g_raw = setup.tile([P, Q_RANK], BF16)
         nc.gpsimd.dma_start(out=g_raw[:], in_=q_a_norm.partition_broadcast(P))
-        nc.gpsimd.tensor_copy(out=g_b[:].rearrange("p (j m) -> p j m", j=4),
-                              in_=g_raw[:].rearrange("p (m j) -> p j m", j=4))
-        ident_b = const.tile([P, P], BF16)
-        make_identity(nc, ident_b[:])
+        nc.gpsimd.tensor_copy(out=g_b[:].rearrange("p (u m e) -> p u m e", u=2, e=2),
+                              in_=g_raw[:].rearrange("p (m u e) -> p u m e", u=2, e=2))
         neg_half = const.tile([P, UNIT], F32)
         nc.gpsimd.memset(neg_half[:], -0.5)
 
@@ -129,8 +127,10 @@ def tile_multiheadlatentattention_pa_t_kernel(tc, x, w_dq, q_a_norm, w_uq, out):
         w_grps = []
         for g in range(2):
             w_grp = setup.tile([P, Q_RANK, 4], BF16, align_bytes=64, name="w_grp%d" % g)
-            nc.vector.tensor_copy(out=w_grp[:].rearrange("p (j m) t -> p j m t", j=4),
-                                  in_=w_raw[:, g, :].rearrange("p (t m j) -> p j m t", t=4, j=4))
+            for u in range(2):
+                nc.vector.tensor_copy(
+                    out=w_grp[:, 2 * P * u:2 * P * (u + 1), :].rearrange("p (m e) t -> p m e t", e=2),
+                    in_=w_raw[:, g, :].rearrange("p (t m u e) -> p u m e t", t=4, u=2, e=2)[:, u])
             w_grps.append(w_grp)
         for g in range(2):
             nc.vector.quantize_mx(out=wdq_c[:, g, :].bitcast(FP8X4), scales=wdq_s[:, g, :],
@@ -206,13 +206,15 @@ def tile_multiheadlatentattention_pa_t_kernel(tc, x, w_dq, q_a_norm, w_uq, out):
 
         def t_h(u, i):
             if i == 0:
-                st["ht", u] = psum.tile([P, UNIT, 4, P], BF16, name="ht", bufs=1)
-            for j in range(4):
-                nc.tensor.transpose(st["ht", u][:, i, j, :], st["h", u][:, i, j * P:(j + 1) * P], ident_b[:])
+                st["ht", u] = psum.tile([P, UNIT, 2, P], F32, name="ht", bufs=1)
+            words = st["h", u][:, i, :].bitcast(F32)
+            for j in range(2):
+                nc.tensor.transpose(st["ht", u][:, i, j, :], words[:, j * P:(j + 1) * P], ident_f[:])
 
         def c_h(u):
             hg = work.tile([P, UNIT, P, 4], BF16, align_bytes=64, name="hg")
-            nc.scalar.copy(out=hg[:], in_=st["ht", u][:].rearrange("p i j w -> p i w j"))
+            nc.scalar.copy(out=hg[:].rearrange("p i w j -> p i (w j)").bitcast(F32).rearrange("p i (w j) -> p i w j", j=2),
+                           in_=st["ht", u][:].rearrange("p i j w -> p i w j"))
             st["hg", u] = hg
 
         def q_h(u):

@@ -28,7 +28,7 @@ AHEAD = 6
 MANUAL = True
 VEC_MOD = 2
 VEC_COPY = ()
-LAG_M1, LAG_NORM, LAG_TH, LAG_CH, LAG_QH, LAG_M2, LAG_ROPE = 3, 4, 5, 5, 5, 6, 7
+LAG_M1, LAG_NORM, LAG_TH, LAG_M2, LAG_ROPE = 2, 3, 4, 5, 6
 
 FLOPS = 2 * B * S * (D * Q_RANK + Q_RANK * NOUT)
 
@@ -265,27 +265,27 @@ def tile_multiheadlatentattention_pa_t_kernel(tc, x, w_dq, q_a_norm, w_uq, out):
         for s in range(UNITS + LAG_ROPE):
             on(rope, s - LAG_ROPE)
             on(norm, s - LAG_NORM)
-            on(mx1, s - LAG_M1, 0)
-            on(s_q, s - LAG_M1, 0)
             on(t_x, s, 0)
-            on(c_x, s, 0)
+            on(t_x, s, 1)
             on(t_h, s - LAG_TH, 0)
             on(t_h, s - LAG_TH, 1)
-            on(c_h, s - LAG_CH)
+            on(mx1, s - LAG_M1, 0)
             on(mx1, s - LAG_M1, 1)
+            on(mx2, s - LAG_M2)
+            on(c_x, s, 0)
+            on(c_x, s, 1)
+            on(c_h, s - LAG_TH)
+            on(s_q, s - LAG_M1, 0)
             on(s_q, s - LAG_M1, 1)
-            if s == LAG_M1:
+            if s == 3:
                 tables_scalar()
             on(r_t, s - LAG_M1)
-            if s == LAG_M1:
+            if s == 3:
                 tables_negate()
-            on(t_x, s, 1)
-            on(mx2, s - LAG_M2)
-            on(c_x, s, 1)
-            on(q_x, s - 1)
+            on(q_x, s)
+            on(q_h, s - LAG_TH)
             if s == 1:
                 tables_vector()
             if s == 2:
                 weights_up()
-            on(q_h, s - LAG_QH)
             on(load, s + AHEAD)

@@ -28,7 +28,7 @@ AHEAD = 6
 MANUAL = True
 VEC_MOD = 2
 VEC_COPY = ()
-LAG_M1, LAG_NORM, LAG_TH, LAG_M2, LAG_ROPE = 2, 3, 4, 5, 6
+LAG_M1, LAG_NORM, LAG_TH, LAG_M2, LAG_ROPE = 1, 2, 3, 4, 5
 
 FLOPS = 2 * B * S * (D * Q_RANK + Q_RANK * NOUT)
 
@@ -55,27 +55,35 @@ def tile_multiheadlatentattention_pa_t_kernel(tc, x, w_dq, q_a_norm, w_uq, out):
         def load(u):
             x_sb = xpool.tile([P, UNIT, D], BF16, name="x_sb")
             b, t0 = u // UPB, (u % UPB) * UNIT
-            nc.sync.dma_start(out=x_sb[:], in_=xv[b, :, t0:t0 + UNIT, :])
+            if u < 2:
+                for i in range(UNIT):
+                    nc.sync.dma_start(out=x_sb[:, i, :], in_=xv[b, :, t0 + i, :])
+            else:
+                nc.sync.dma_start(out=x_sb[:], in_=xv[b, :, t0:t0 + UNIT, :])
             st["x", u] = x_sb
 
         w_raw = setup.tile([P, 2, 4 * Q_RANK], BF16)
         w_view = w_dq.rearrange("(g p t) c -> p g (t c)", g=2, p=P, t=4)
+        g_row = setup.tile([P, Q_RANK], BF16)
+        nc.gpsimd.memset(g_row[:], 0.0)
+        load(0)
+        nc.sync.dma_start(out=g_row[0:1, :], in_=q_a_norm.rearrange("(o c) -> o c", o=1))
         nc.sync.dma_start(out=w_raw[:, 0, :], in_=w_view[:, 0, :])
+        load(1)
         nc.sync.dma_start(out=w_raw[:, 1, :], in_=w_view[:, 1, :])
-        for u in range(AHEAD):
-            load(u)
+        load(2)
         u_raw = setup.tile([P, 4, NOUT], BF16)
-        nc.scalar.dma_start(out=u_raw[:], in_=w_uq.rearrange("(p j) n -> p j n", j=4))
+        nc.sync.dma_start(out=u_raw[:], in_=w_uq.rearrange("(p j) n -> p j n", j=4))
+        for u in range(3, AHEAD):
+            load(u)
 
         pos_i = setup.tile([P, TPB], I32)
         nc.gpsimd.iota(pos_i[:], pattern=[[1, TPB]], base=0, channel_multiplier=TPB)
         ident_f = const.tile([P, P], F32)
         make_identity(nc, ident_f[:])
         g_b = const.tile([P, Q_RANK], BF16)
-        g_raw = setup.tile([P, Q_RANK], BF16)
-        nc.gpsimd.dma_start(out=g_raw[:], in_=q_a_norm.partition_broadcast(P))
-        nc.gpsimd.tensor_copy(out=g_b[:].rearrange("p (u m e) -> p u m e", u=2, e=2),
-                              in_=g_raw[:].rearrange("p (m u e) -> p u m e", u=2, e=2))
+        ones = setup.tile([P, P], BF16)
+        nc.gpsimd.memset(ones[:], 1.0)
         neg_half = const.tile([P, UNIT], F32)
         nc.gpsimd.memset(neg_half[:], -0.5)
 
@@ -100,8 +108,7 @@ def tile_multiheadlatentattention_pa_t_kernel(tc, x, w_dq, q_a_norm, w_uq, out):
                                 scalar2=None, op0=ALU.bitwise_and)
         frac = setup.tile([P, 2, TPB * HALF], F32)
         negf = setup.tile([P, 2, HALF, TPB], F32)
-        cos_t = const.tile([P, TPB, HALF], F32)
-        sin_t = const.tile([P, TPB, 2, HALF], F32)
+        trig = const.tile([P, TPB, 2, ROPE], F32)
 
         def tables_vector():
             nc.vector.scalar_tensor_tensor(
@@ -114,27 +121,28 @@ def tile_multiheadlatentattention_pa_t_kernel(tc, x, w_dq, q_a_norm, w_uq, out):
 
         def tables_scalar():
             by_pos = negf[:].rearrange("p a i t -> p a t i")
-            nc.scalar.activation(out=cos_t[:], in_=by_pos[:, 1], func=ACT.Sin, scale=-2.0 * math.pi, bias=-math.pi)
-            nc.scalar.activation(out=sin_t[:, :, 0, :], in_=by_pos[:, 0], func=ACT.Sin,
-                                 scale=-2.0 * math.pi, bias=-math.pi)
+            for a in range(2):
+                nc.scalar.activation(out=trig[:, :, a, 0:HALF], in_=by_pos[:, 1 - a], func=ACT.Sin,
+                                     scale=-2.0 * math.pi, bias=-math.pi)
 
-        def tables_negate():
-            nc.gpsimd.tensor_scalar(out=sin_t[:, :, 1, :], in0=sin_t[:, :, 0, :], scalar1=-1.0, scalar2=0.0,
-                                    op0=ALU.mult, op1=ALU.add)
+        def tables_spread(a):
+            nc.gpsimd.tensor_scalar(out=trig[:, :, a, HALF:], in0=trig[:, :, a, 0:HALF],
+                                    scalar1=1.0 - 2.0 * a, scalar2=0.0, op0=ALU.mult, op1=ALU.add)
 
         wdq_c = const.tile([P, 2, Q_RANK], U32, align_bytes=64)
         wdq_s = const.tile([P, 2, Q_RANK], U8, align_bytes=64)
         w_grps = []
-        for g in range(2):
-            w_grp = setup.tile([P, Q_RANK, 4], BF16, align_bytes=64, name="w_grp%d" % g)
-            for u in range(2):
-                nc.vector.tensor_copy(
-                    out=w_grp[:, 2 * P * u:2 * P * (u + 1), :].rearrange("p (m e) t -> p m e t", e=2),
-                    in_=w_raw[:, g, :].rearrange("p (t m u e) -> p u m e t", t=4, u=2, e=2)[:, u])
-            w_grps.append(w_grp)
-        for g in range(2):
+
+        def weights_copy(g, u, copy):
+            if u == 0:
+                w_grps.append(setup.tile([P, Q_RANK, 4], BF16, align_bytes=64, name="w_grp%d" % g))
+            copy(out=w_grps[g][:, 2 * P * u:2 * P * (u + 1), :].rearrange("p (m e) t -> p m e t", e=2),
+                 in_=w_raw[:, g, :].rearrange("p (t m u e) -> p u m e t", t=4, u=2, e=2)[:, u])
+
+        def weights_quantise(g):
             nc.vector.quantize_mx(out=wdq_c[:, g, :].bitcast(FP8X4), scales=wdq_s[:, g, :],
                                   in_=w_grps[g][:].rearrange("p c t -> p (c t)"))
+
         wuq_c = const.tile([P, NOUT], U32, align_bytes=64)
         wuq_s = const.tile([P, NOUT], U8, align_bytes=64)
         u_grp = setup.tile([P, 2, H, NOPE, 4], BF16, align_bytes=64)
@@ -142,7 +150,10 @@ def tile_multiheadlatentattention_pa_t_kernel(tc, x, w_dq, q_a_norm, w_uq, out):
         def weights_up():
             u_src = u_raw[:].rearrange("p j (h r f) -> p r h f j", h=H, r=2)
             for r in range(2):
-                nc.vector.tensor_copy(out=u_grp[:, r], in_=u_src[:, r])
+                nc.gpsimd.tensor_scalar(out=u_grp[:, r], in0=u_src[:, r], scalar1=1.0, scalar2=0.0,
+                                        op0=ALU.mult, op1=ALU.add)
+
+        def weights_up_quantise():
             nc.vector.quantize_mx(out=wuq_c[:].bitcast(FP8X4), scales=wuq_s[:],
                                   in_=u_grp[:].rearrange("p r h f j -> p (r h f j)"))
 
@@ -237,32 +248,40 @@ def tile_multiheadlatentattention_pa_t_kernel(tc, x, w_dq, q_a_norm, w_uq, out):
             q_ps = st["q", u]
             b, t0 = u // UPB, (u % UPB) * UNIT
             o_sb = work.tile([P, UNIT, H, QK], F32, name="o_sb", bufs=4)
-            by_cos = work.tile([P, UNIT, H, 2, HALF], F32, name="by_cos")
-            by_sin = work.tile([P, UNIT, H, 2, HALF], F32, name="by_sin")
+            prod = work.tile([P, UNIT, 2, H, ROPE], F32, name="prod")
             nc.vector.tensor_tensor(
-                out=by_cos[:].rearrange("p i h r f -> p i (h r) f"),
-                in0=q_ps[:, :, H * NOPE:].rearrange("p i (a f) -> p i a f", f=HALF),
-                in1=cos_t[:, t0:t0 + UNIT, :].unsqueeze(2).to_broadcast([P, UNIT, 2 * H, HALF]),
-                op=ALU.mult)
-            nc.vector.tensor_tensor(
-                out=by_sin[:].rearrange("p i h r f -> p i h (r f)"),
-                in0=q_ps[:, :, H * NOPE:].rearrange("p i (h f) -> p i h f", h=H),
-                in1=sin_t[:, t0:t0 + UNIT].rearrange("p i r f -> p i (r f)").unsqueeze(2).to_broadcast(
-                    [P, UNIT, H, ROPE]),
+                out=prod[:],
+                in0=q_ps[:, :, H * NOPE:].rearrange("p i (h f) -> p i h f", h=H).unsqueeze(2).to_broadcast(
+                    [P, UNIT, 2, H, ROPE]),
+                in1=trig[:, t0:t0 + UNIT].unsqueeze(3).to_broadcast([P, UNIT, 2, H, ROPE]),
                 op=ALU.mult)
             nc.vector.tensor_copy(out=o_sb[:, :, :, 0:NOPE],
                                   in_=q_ps[:, :, 0:H * NOPE].rearrange("p i (h f) -> p i h f", h=H))
             adder = nc.vector if u == UNITS - 1 else nc.gpsimd
             for r in range(2):
                 adder.tensor_tensor(out=o_sb[:, :, :, NOPE + r * HALF:NOPE + (r + 1) * HALF],
-                                        in0=by_cos[:, :, :, r, :], in1=by_sin[:, :, :, 1 - r, :], op=ALU.add)
+                                        in0=prod[:, :, 0, :, r * HALF:(r + 1) * HALF],
+                                    in1=prod[:, :, 1, :, (1 - r) * HALF:(2 - r) * HALF], op=ALU.add)
             nc.sync.dma_start(out=ov[b, :, t0:t0 + UNIT, :], in_=o_sb[:].rearrange("p i h f -> p i (h f)"))
+
+        def gain_spread():
+            g_ps = psum.tile([P, Q_RANK], F32, name="c_ps", bufs=4)
+            nc.tensor.matmul(g_ps[:], lhsT=ones[:], rhs=g_row[:], start=True, stop=True)
+            nc.scalar.copy(out=g_b[:].rearrange("p (u m e) -> p u m e", u=2, e=2),
+                           in_=g_ps[:].rearrange("p (m u e) -> p u m e", u=2, e=2))
 
         def on(fn, u, *half):
             if 0 <= u < UNITS:
                 fn(u, *half)
 
         for s in range(UNITS + LAG_ROPE):
+            if s == 1:
+                weights_copy(0, 1, nc.scalar.copy)
+                weights_quantise(0)
+                weights_copy(1, 0, nc.vector.tensor_copy)
+                weights_copy(1, 1, nc.scalar.copy)
+                weights_quantise(1)
+                weights_up()
             on(rope, s - LAG_ROPE)
             on(norm, s - LAG_NORM)
             on(t_x, s, 0)
@@ -277,15 +296,18 @@ def tile_multiheadlatentattention_pa_t_kernel(tc, x, w_dq, q_a_norm, w_uq, out):
             on(c_h, s - LAG_TH)
             on(s_q, s - LAG_M1, 0)
             on(s_q, s - LAG_M1, 1)
-            if s == 3:
+            if s == 2:
                 tables_scalar()
             on(r_t, s - LAG_M1)
-            if s == 3:
-                tables_negate()
+            if 2 <= s <= 3:
+                tables_spread(s - 2)
+            if s == 0:
+                gain_spread()
+                weights_copy(0, 0, nc.vector.tensor_copy)
             on(q_x, s)
-            on(q_h, s - LAG_TH)
             if s == 1:
                 tables_vector()
+            on(q_h, s - LAG_TH)
             if s == 2:
-                weights_up()
+                weights_up_quantise()
             on(load, s + AHEAD)

@@ -28,7 +28,7 @@ AHEAD = 6
 MANUAL = True
 VEC_MOD = 2
 VEC_COPY = ()
-LAG_M1, LAG_NORM, LAG_TH, LAG_M2, LAG_ROPE = 1, 2, 3, 4, 5
+LAG_QX, LAG_M1, LAG_NORM, LAG_TH, LAG_M2, LAG_ROPE = 1, 2, 3, 4, 5, 6
 
 FLOPS = 2 * B * S * (D * Q_RANK + Q_RANK * NOUT)
 
@@ -275,6 +275,8 @@ def tile_multiheadlatentattention_pa_t_kernel(tc, x, w_dq, q_a_norm, w_uq, out):
                 fn(u, *half)
 
         for s in range(UNITS + LAG_ROPE):
+            on(rope, s - LAG_ROPE)
+            on(q_x, s - LAG_QX)
             if s == 1:
                 weights_copy(0, 1, nc.scalar.copy)
                 weights_quantise(0)
@@ -282,7 +284,8 @@ def tile_multiheadlatentattention_pa_t_kernel(tc, x, w_dq, q_a_norm, w_uq, out):
                 weights_copy(1, 1, nc.scalar.copy)
                 weights_quantise(1)
                 weights_up()
-            on(rope, s - LAG_ROPE)
+            if s == 2:
+                tables_vector()
             on(norm, s - LAG_NORM)
             on(t_x, s, 0)
             on(t_x, s, 1)
@@ -296,18 +299,15 @@ def tile_multiheadlatentattention_pa_t_kernel(tc, x, w_dq, q_a_norm, w_uq, out):
             on(c_h, s - LAG_TH)
             on(s_q, s - LAG_M1, 0)
             on(s_q, s - LAG_M1, 1)
-            if s == 2:
+            if s == 3:
                 tables_scalar()
             on(r_t, s - LAG_M1)
-            if 2 <= s <= 3:
-                tables_spread(s - 2)
+            if 3 <= s <= 4:
+                tables_spread(s - 3)
             if s == 0:
                 gain_spread()
                 weights_copy(0, 0, nc.vector.tensor_copy)
-            on(q_x, s)
-            if s == 1:
-                tables_vector()
             on(q_h, s - LAG_TH)
-            if s == 2:
+            if s == 3:
                 weights_up_quantise()
             on(load, s + AHEAD)

@@ -25,14 +25,9 @@ UNIT = 2
 UPB = TPB // UNIT
 UNITS = B * UPB
 AHEAD = 6
-MANUAL = True
-VEC_MOD = 2
-VEC_COPY = ()
 LAG_QX, LAG_M1, LAG_NORM, LAG_TH, LAG_M2, LAG_ROPE = 1, 2, 3, 4, 5, 6
 
 FLOPS = 2 * B * S * (D * Q_RANK + Q_RANK * NOUT)
-
-GRID = 2 ** 15
 
 
 def tile_multiheadlatentattention_pa_t_kernel(tc, x, w_dq, q_a_norm, w_uq, out):
@@ -47,9 +42,7 @@ def tile_multiheadlatentattention_pa_t_kernel(tc, x, w_dq, q_a_norm, w_uq, out):
         work = ctx.enter_context(tc.tile_pool(name="work", bufs=3))
         small = ctx.enter_context(tc.tile_pool(name="small", bufs=4))
         psum = ctx.enter_context(tc.psum_pool(name="psum", bufs=1))
-        if MANUAL:
-            ctx.enter_context(tc.manual_schedule())
-
+        ctx.enter_context(tc.manual_schedule())
         st = {}
 
         def load(u):
@@ -93,41 +86,33 @@ def tile_multiheadlatentattention_pa_t_kernel(tc, x, w_dq, q_a_norm, w_uq, out):
         nc.scalar.activation(out=warm[:], in_=zero[:], func=ACT.Sin)
         pos_f = setup.tile([P, TPB], F32)
         nc.vector.tensor_copy(out=pos_f[:], in_=pos_i[:])
-        turn_i = setup.tile([P, 2, HALF, TPB], I32)
-        turn_lo = setup.tile([P, HALF, TPB], F32)
+        turns = setup.tile([P, HALF, TPB], F32)
         for i in range(HALF):
             freq = 1.0 / THETA ** (i / HALF) / (2.0 * math.pi)
-            f_hi = math.floor(freq * GRID)
-            f_lo = freq - f_hi / GRID
-            nc.vector.tensor_scalar(out=turn_i[:, 0, i, :], in0=pos_f[:], scalar1=float(f_hi),
-                                    scalar2=float(GRID // 2), op0=ALU.mult, op1=ALU.add)
-            nc.scalar.activation(out=turn_lo[:, i, :], in_=pos_f[:], func=ACT.Copy, scale=f_lo)
-        nc.vector.tensor_scalar(out=turn_i[:, 1], in0=turn_i[:, 0], scalar1=float(GRID // 4),
-                                scalar2=None, op0=ALU.add)
-        nc.vector.tensor_scalar(out=turn_i[:], in0=turn_i[:], scalar1=GRID - 1,
-                                scalar2=None, op0=ALU.bitwise_and)
-        frac = setup.tile([P, 2, TPB * HALF], F32)
-        negf = setup.tile([P, 2, HALF, TPB], F32)
+            if i < HALF // 2:
+                nc.vector.tensor_scalar(out=turns[:, i, :], in0=pos_f[:], scalar1=freq, scalar2=None, op0=ALU.mult)
+            else:
+                nc.scalar.activation(out=turns[:, i, :], in_=pos_f[:], func=ACT.Copy, scale=freq)
+        whole = setup.tile([P, HALF, TPB], I32)
+        part = setup.tile([P, HALF, TPB], F32)
+        frac = setup.tile([P, HALF, TPB], F32)
+        size = setup.tile([P, TPB, HALF], F32)
         trig = const.tile([P, TPB, 2, ROPE], F32)
 
-        def tables_vector():
-            nc.vector.scalar_tensor_tensor(
-                out=frac[:], in0=turn_i[:].rearrange("p a i t -> p a (i t)"), scalar=1.0 / GRID,
-                in1=turn_lo[:].rearrange("p i t -> p (i t)").unsqueeze(1).to_broadcast([P, 2, TPB * HALF]),
-                op0=ALU.mult, op1=ALU.add)
-            nc.vector.scalar_tensor_tensor(
-                out=negf[:].rearrange("p a i t -> p a (i t)"), in0=frac[:], scalar=1.0, in1=frac[:],
-                op0=ALU.is_ge, op1=ALU.subtract)
+        nc.vector.tensor_copy(out=whole[:], in_=turns[:])
+        nc.vector.tensor_tensor(out=part[:], in0=turns[:], in1=whole[:], op=ALU.subtract)
+        nc.vector.scalar_tensor_tensor(out=frac[:], in0=part[:], scalar=0.0, in1=part[:],
+                                       op0=ALU.is_lt, op1=ALU.add)
 
-        def tables_scalar():
-            by_pos = negf[:].rearrange("p a i t -> p a t i")
+        def tables():
+            by_pos = frac[:].rearrange("p i t -> p t i")
+            nc.scalar.activation(out=size[:], in_=by_pos, func=ACT.Abs, scale=-2.0 * math.pi, bias=math.pi)
+            nc.scalar.activation(out=trig[:, :, 0, 0:HALF], in_=size[:], func=ACT.Sin, bias=-math.pi / 2.0)
+            nc.scalar.activation(out=trig[:, :, 1, 0:HALF], in_=by_pos, func=ACT.Sin, scale=-2.0 * math.pi,
+                                 bias=math.pi)
             for a in range(2):
-                nc.scalar.activation(out=trig[:, :, a, 0:HALF], in_=by_pos[:, 1 - a], func=ACT.Sin,
-                                     scale=-2.0 * math.pi, bias=-math.pi)
-
-        def tables_spread(a):
-            nc.gpsimd.tensor_scalar(out=trig[:, :, a, HALF:], in0=trig[:, :, a, 0:HALF],
-                                    scalar1=1.0 - 2.0 * a, scalar2=0.0, op0=ALU.mult, op1=ALU.add)
+                nc.gpsimd.tensor_scalar(out=trig[:, :, a, HALF:], in0=trig[:, :, a, 0:HALF],
+                                        scalar1=1.0 - 2.0 * a, scalar2=0.0, op0=ALU.mult, op1=ALU.add)
 
         wdq_c = const.tile([P, 2, Q_RANK], U32, align_bytes=64)
         wdq_s = const.tile([P, 2, Q_RANK], U8, align_bytes=64)
@@ -150,8 +135,7 @@ def tile_multiheadlatentattention_pa_t_kernel(tc, x, w_dq, q_a_norm, w_uq, out):
         def weights_up():
             u_src = u_raw[:].rearrange("p j (h r f) -> p r h f j", h=H, r=2)
             for r in range(2):
-                nc.gpsimd.tensor_scalar(out=u_grp[:, r], in0=u_src[:, r], scalar1=1.0, scalar2=0.0,
-                                        op0=ALU.mult, op1=ALU.add)
+                nc.vector.tensor_copy(out=u_grp[:, r], in_=u_src[:, r])
 
         def weights_up_quantise():
             nc.vector.quantize_mx(out=wuq_c[:].bitcast(FP8X4), scales=wuq_s[:],
@@ -170,10 +154,7 @@ def tile_multiheadlatentattention_pa_t_kernel(tc, x, w_dq, q_a_norm, w_uq, out):
         def c_x(u, i):
             planes = st["xt", u, i][:].rearrange("p (g u) w -> p g w u", u=2)
             dst = st["xg", u][:, i].bitcast(F32)
-            if i == 1 and u % VEC_MOD in VEC_COPY and u < UNITS - 1:
-                nc.vector.tensor_copy(out=dst, in_=planes)
-            else:
-                nc.scalar.copy(out=dst, in_=planes)
+            nc.scalar.copy(out=dst, in_=planes)
 
         def q_x(u):
             xc = work.tile([P, UNIT * 2 * P], U32, align_bytes=64, name="xc", bufs=5)
@@ -237,7 +218,10 @@ def tile_multiheadlatentattention_pa_t_kernel(tc, x, w_dq, q_a_norm, w_uq, out):
 
         def mx2(u):
             hc, hs = st["hc", u]
-            q_ps = psum.tile([P, UNIT, NOUT], F32, name="q_ps", bufs=1)
+            if u == UNITS - 1:
+                q_ps = psum.tile([P, 4, P], F32, name="xt", bufs=2)[:].rearrange("p (i r) w -> p i (r w)", i=UNIT)
+            else:
+                q_ps = psum.tile([P, UNIT, NOUT], F32, name="q_ps", bufs=1)
             for i in range(UNIT):
                 cols = slice(i * P, (i + 1) * P)
                 nc.tensor.matmul_mx(out=q_ps[:, i, :], lhsT=hc[:, cols].bitcast(FP8X4), lhsT_scale=hs[:, cols],
@@ -260,7 +244,7 @@ def tile_multiheadlatentattention_pa_t_kernel(tc, x, w_dq, q_a_norm, w_uq, out):
             adder = nc.vector if u == UNITS - 1 else nc.gpsimd
             for r in range(2):
                 adder.tensor_tensor(out=o_sb[:, :, :, NOPE + r * HALF:NOPE + (r + 1) * HALF],
-                                        in0=prod[:, :, 0, :, r * HALF:(r + 1) * HALF],
+                                    in0=prod[:, :, 0, :, r * HALF:(r + 1) * HALF],
                                     in1=prod[:, :, 1, :, (1 - r) * HALF:(2 - r) * HALF], op=ALU.add)
             nc.sync.dma_start(out=ov[b, :, t0:t0 + UNIT, :], in_=o_sb[:].rearrange("p i h f -> p i (h f)"))
 
@@ -281,11 +265,8 @@ def tile_multiheadlatentattention_pa_t_kernel(tc, x, w_dq, q_a_norm, w_uq, out):
                 weights_copy(0, 1, nc.scalar.copy)
                 weights_quantise(0)
                 weights_copy(1, 0, nc.vector.tensor_copy)
-                weights_copy(1, 1, nc.scalar.copy)
+                weights_copy(1, 1, nc.vector.tensor_copy)
                 weights_quantise(1)
-                weights_up()
-            if s == 2:
-                tables_vector()
             on(norm, s - LAG_NORM)
             on(t_x, s, 0)
             on(t_x, s, 1)
@@ -297,13 +278,13 @@ def tile_multiheadlatentattention_pa_t_kernel(tc, x, w_dq, q_a_norm, w_uq, out):
             on(c_x, s, 0)
             on(c_x, s, 1)
             on(c_h, s - LAG_TH)
+            if s == 1:
+                tables()
+            if s == 2:
+                weights_up()
             on(s_q, s - LAG_M1, 0)
             on(s_q, s - LAG_M1, 1)
-            if s == 3:
-                tables_scalar()
             on(r_t, s - LAG_M1)
-            if 3 <= s <= 4:
-                tables_spread(s - 3)
             if s == 0:
                 gain_spread()
                 weights_copy(0, 0, nc.vector.tensor_copy)

@@ -77,8 +77,6 @@ def tile_multiheadlatentattention_pa_t_kernel(tc, x, w_dq, q_a_norm, w_uq, out):
         g_b = const.tile([P, Q_RANK], BF16)
         ones = setup.tile([P, P], BF16)
         nc.gpsimd.memset(ones[:], 1.0)
-        neg_half = const.tile([P, UNIT], F32)
-        nc.gpsimd.memset(neg_half[:], -0.5)
 
         zero = setup.tile([P, 1], F32)
         nc.vector.memset(zero[:], 0.0)
@@ -95,24 +93,27 @@ def tile_multiheadlatentattention_pa_t_kernel(tc, x, w_dq, q_a_norm, w_uq, out):
                 nc.scalar.activation(out=turns[:, i, :], in_=pos_f[:], func=ACT.Copy, scale=freq)
         whole = setup.tile([P, HALF, TPB], I32)
         part = setup.tile([P, HALF, TPB], F32)
-        frac = setup.tile([P, HALF, TPB], F32)
-        size = setup.tile([P, TPB, HALF], F32)
+        half = setup.tile([P, TPB, HALF], F32)
+        half_sq = setup.tile([P, TPB, HALF], F32)
         trig = const.tile([P, TPB, 2, ROPE], F32)
 
         nc.vector.tensor_copy(out=whole[:], in_=turns[:])
         nc.vector.tensor_tensor(out=part[:], in0=turns[:], in1=whole[:], op=ALU.subtract)
-        nc.vector.scalar_tensor_tensor(out=frac[:], in0=part[:], scalar=0.0, in1=part[:],
-                                       op0=ALU.is_lt, op1=ALU.add)
+
+        by_pos = part[:].rearrange("p i t -> p t i")
+
+        def sine_half():
+            nc.scalar.activation(out=half[:], in_=by_pos, func=ACT.Sin, scale=math.pi)
 
         def tables():
-            by_pos = frac[:].rearrange("p i t -> p t i")
-            nc.scalar.activation(out=size[:], in_=by_pos, func=ACT.Abs, scale=-2.0 * math.pi, bias=math.pi)
-            nc.scalar.activation(out=trig[:, :, 0, 0:HALF], in_=size[:], func=ACT.Sin, bias=-math.pi / 2.0)
-            nc.scalar.activation(out=trig[:, :, 1, 0:HALF], in_=by_pos, func=ACT.Sin, scale=-2.0 * math.pi,
-                                 bias=math.pi)
-            for a in range(2):
-                nc.gpsimd.tensor_scalar(out=trig[:, :, a, HALF:], in0=trig[:, :, a, 0:HALF],
-                                        scalar1=1.0 - 2.0 * a, scalar2=0.0, op0=ALU.mult, op1=ALU.add)
+            nc.scalar.activation(out=trig[:, :, 1, 0:HALF], in_=by_pos, func=ACT.Sin, scale=2.0 * math.pi)
+            nc.scalar.activation(out=warm[:], in_=zero[:], func=ACT.Abs_reciprocal_sqrt, bias=1.0)
+            nc.gpsimd.tensor_tensor(out=half_sq[:], in0=half[:], in1=half[:], op=ALU.mult)
+            for r in range(2):
+                nc.gpsimd.tensor_scalar(out=trig[:, :, 0, r * HALF:(r + 1) * HALF], in0=half_sq[:],
+                                        scalar1=-2.0, scalar2=1.0, op0=ALU.mult, op1=ALU.add)
+            nc.gpsimd.tensor_scalar(out=trig[:, :, 1, HALF:], in0=trig[:, :, 1, 0:HALF],
+                                    scalar1=-1.0, scalar2=0.0, op0=ALU.mult, op1=ALU.add)
 
         wdq_c = const.tile([P, 2, Q_RANK], U32, align_bytes=64)
         wdq_s = const.tile([P, 2, Q_RANK], U8, align_bytes=64)
@@ -181,11 +182,9 @@ def tile_multiheadlatentattention_pa_t_kernel(tc, x, w_dq, q_a_norm, w_uq, out):
                                  accum_out=st["ss", u][:, i:i + 1])
 
         def r_t(u):
-            ms = small.tile([P, UNIT], F32, name="ms")
-            nc.gpsimd.tensor_scalar(out=ms[:], in0=st["ss", u][:], scalar1=1.0 / Q_RANK, scalar2=EPS,
-                                    op0=ALU.mult, op1=ALU.add)
             rstd = small.tile([P, UNIT], F32, name="rstd")
-            nc.gpsimd.tensor_tensor(out=rstd[:], in0=ms[:], in1=neg_half[:], op=ALU.pow)
+            nc.scalar.activation(out=rstd[:], in_=st["ss", u][:], func=ACT.Abs_reciprocal_sqrt, scale=1.0 / Q_RANK,
+                                 bias=EPS)
             st["rstd", u] = rstd
 
         def norm(u):
@@ -232,7 +231,7 @@ def tile_multiheadlatentattention_pa_t_kernel(tc, x, w_dq, q_a_norm, w_uq, out):
             q_ps = st["q", u]
             b, t0 = u // UPB, (u % UPB) * UNIT
             o_sb = work.tile([P, UNIT, H, QK], F32, name="o_sb", bufs=4)
-            prod = work.tile([P, UNIT, 2, H, ROPE], F32, name="prod")
+            prod = work.tile([P, UNIT, 2, H, ROPE], F32, name="prod", bufs=UNITS)
             nc.vector.tensor_tensor(
                 out=prod[:],
                 in0=q_ps[:, :, H * NOPE:].rearrange("p i (h f) -> p i h f", h=H).unsqueeze(2).to_broadcast(
@@ -249,25 +248,25 @@ def tile_multiheadlatentattention_pa_t_kernel(tc, x, w_dq, q_a_norm, w_uq, out):
             nc.sync.dma_start(out=ov[b, :, t0:t0 + UNIT, :], in_=o_sb[:].rearrange("p i h f -> p i (h f)"))
 
         def gain_spread():
-            g_ps = psum.tile([P, Q_RANK], F32, name="c_ps", bufs=4)
-            nc.tensor.matmul(g_ps[:], lhsT=ones[:], rhs=g_row[:], start=True, stop=True)
-            nc.scalar.copy(out=g_b[:].rearrange("p (u m e) -> p u m e", u=2, e=2),
-                           in_=g_ps[:].rearrange("p (m u e) -> p u m e", u=2, e=2))
+            st["g"] = psum.tile([P, Q_RANK], F32, name="c_ps", bufs=4)
+            nc.tensor.matmul(st["g"][:], lhsT=ones[:], rhs=g_row[:], start=True, stop=True)
 
-        def on(fn, u, *half):
+        def gain_copy():
+            nc.scalar.copy(out=g_b[:].rearrange("p (u m e) -> p u m e", u=2, e=2),
+                           in_=st["g"][:].rearrange("p (m u e) -> p u m e", u=2, e=2))
+
+        def on(fn, u, *which):
             if 0 <= u < UNITS:
-                fn(u, *half)
+                fn(u, *which)
 
         for s in range(UNITS + LAG_ROPE):
             on(rope, s - LAG_ROPE)
             on(q_x, s - LAG_QX)
             if s == 1:
-                weights_copy(0, 1, nc.scalar.copy)
                 weights_quantise(0)
                 weights_copy(1, 0, nc.vector.tensor_copy)
                 weights_copy(1, 1, nc.vector.tensor_copy)
                 weights_quantise(1)
-            on(norm, s - LAG_NORM)
             on(t_x, s, 0)
             on(t_x, s, 1)
             on(t_h, s - LAG_TH, 0)
@@ -276,19 +275,23 @@ def tile_multiheadlatentattention_pa_t_kernel(tc, x, w_dq, q_a_norm, w_uq, out):
             on(mx1, s - LAG_M1, 1)
             on(mx2, s - LAG_M2)
             on(c_x, s, 0)
+            on(r_t, s - LAG_NORM)
+            on(norm, s - LAG_NORM)
             on(c_x, s, 1)
             on(c_h, s - LAG_TH)
+            if s == 0:
+                gain_spread()
+                weights_copy(0, 0, nc.vector.tensor_copy)
+                weights_copy(0, 1, nc.scalar.copy)
+                sine_half()
             if s == 1:
+                gain_copy()
                 tables()
             if s == 2:
                 weights_up()
             on(s_q, s - LAG_M1, 0)
             on(s_q, s - LAG_M1, 1)
-            on(r_t, s - LAG_M1)
-            if s == 0:
-                gain_spread()
-                weights_copy(0, 0, nc.vector.tensor_copy)
-            on(q_h, s - LAG_TH)
             if s == 3:
                 weights_up_quantise()
+            on(q_h, s - LAG_TH)
             on(load, s + AHEAD)

@@ -24,7 +24,7 @@ TPB = S // P
 UNIT = 2
 UPB = TPB // UNIT
 UNITS = B * UPB
-AHEAD = 6
+AHEAD = 4
 LAG_QX, LAG_M1, LAG_NORM, LAG_TH, LAG_M2, LAG_ROPE = 1, 2, 3, 4, 5, 6
 
 FLOPS = 2 * B * S * (D * Q_RANK + Q_RANK * NOUT)
@@ -38,7 +38,7 @@ def tile_multiheadlatentattention_pa_t_kernel(tc, x, w_dq, q_a_norm, w_uq, out):
     with ExitStack() as ctx:
         const = ctx.enter_context(tc.tile_pool(name="const", bufs=1))
         setup = ctx.enter_context(tc.tile_pool(name="setup", bufs=1))
-        xpool = ctx.enter_context(tc.tile_pool(name="xpool", bufs=AHEAD + 1))
+        xpool = ctx.enter_context(tc.tile_pool(name="xpool", bufs=AHEAD // 2 + 1))
         work = ctx.enter_context(tc.tile_pool(name="work", bufs=3))
         small = ctx.enter_context(tc.tile_pool(name="small", bufs=4))
         psum = ctx.enter_context(tc.psum_pool(name="psum", bufs=1))
@@ -46,14 +46,18 @@ def tile_multiheadlatentattention_pa_t_kernel(tc, x, w_dq, q_a_norm, w_uq, out):
         st = {}
 
         def load(u):
-            x_sb = xpool.tile([P, UNIT, D], BF16, name="x_sb")
             b, t0 = u // UPB, (u % UPB) * UNIT
+            if u % 2 == 0:
+                st["xx", u // 2] = xpool.tile([P, 2, UNIT, D], BF16, name="x_sb")
+            x_sb = st["xx", u // 2]
+            st["x", u] = x_sb[:, u % 2]
             if u < 2:
                 for i in range(UNIT):
-                    nc.sync.dma_start(out=x_sb[:, i, :], in_=xv[b, :, t0 + i, :])
-            else:
-                nc.sync.dma_start(out=x_sb[:], in_=xv[b, :, t0:t0 + UNIT, :])
-            st["x", u] = x_sb
+                    nc.sync.dma_start(out=x_sb[:, u, i, :], in_=xv[b, :, t0 + i, :])
+            elif u < AHEAD:
+                nc.sync.dma_start(out=x_sb[:, u % 2], in_=xv[b, :, t0:t0 + UNIT, :])
+            elif u % 2 == 0:
+                nc.sync.dma_start(out=x_sb[:].rearrange("p e i k -> p (e i) k"), in_=xv[b, :, t0:t0 + 2 * UNIT, :])
 
         w_raw = setup.tile([P, 2, 4 * Q_RANK], BF16)
         w_view = w_dq.rearrange("(g p t) c -> p g (t c)", g=2, p=P, t=4)
@@ -92,25 +96,27 @@ def tile_multiheadlatentattention_pa_t_kernel(tc, x, w_dq, q_a_norm, w_uq, out):
             else:
                 nc.scalar.activation(out=turns[:, i, :], in_=pos_f[:], func=ACT.Copy, scale=freq)
         whole = setup.tile([P, HALF, TPB], I32)
-        part = setup.tile([P, HALF, TPB], F32)
+        part = setup.tile([P, TPB, HALF], F32)
         half = setup.tile([P, TPB, HALF], F32)
-        half_sq = setup.tile([P, TPB, HALF], F32)
         trig = const.tile([P, TPB, 2, ROPE], F32)
 
         nc.vector.tensor_copy(out=whole[:], in_=turns[:])
-        nc.vector.tensor_tensor(out=part[:], in0=turns[:], in1=whole[:], op=ALU.subtract)
-
-        by_pos = part[:].rearrange("p i t -> p t i")
+        nc.vector.tensor_tensor(out=part[:], in0=turns[:].rearrange("p i t -> p t i"),
+                                in1=whole[:].rearrange("p i t -> p t i"), op=ALU.subtract)
 
         def sine_half():
-            nc.scalar.activation(out=half[:], in_=by_pos, func=ACT.Sin, scale=math.pi)
+            nc.scalar.activation(out=half[:], in_=part[:], func=ACT.Sin, scale=math.pi)
+
+        def sine():
+            nc.scalar.activation(out=trig[:, :, 1, 0:HALF], in_=part[:], func=ACT.Sin, scale=2.0 * math.pi)
+
+        def root_table():
+            nc.scalar.activation(out=warm[:], in_=zero[:], func=ACT.Abs_reciprocal_sqrt, bias=1.0)
 
         def tables():
-            nc.scalar.activation(out=trig[:, :, 1, 0:HALF], in_=by_pos, func=ACT.Sin, scale=2.0 * math.pi)
-            nc.scalar.activation(out=warm[:], in_=zero[:], func=ACT.Abs_reciprocal_sqrt, bias=1.0)
-            nc.gpsimd.tensor_tensor(out=half_sq[:], in0=half[:], in1=half[:], op=ALU.mult)
+            nc.gpsimd.tensor_tensor(out=half[:], in0=half[:], in1=half[:], op=ALU.mult)
             for r in range(2):
-                nc.gpsimd.tensor_scalar(out=trig[:, :, 0, r * HALF:(r + 1) * HALF], in0=half_sq[:],
+                nc.gpsimd.tensor_scalar(out=trig[:, :, 0, r * HALF:(r + 1) * HALF], in0=half[:],
                                         scalar1=-2.0, scalar2=1.0, op0=ALU.mult, op1=ALU.add)
             nc.gpsimd.tensor_scalar(out=trig[:, :, 1, HALF:], in0=trig[:, :, 1, 0:HALF],
                                     scalar1=-1.0, scalar2=0.0, op0=ALU.mult, op1=ALU.add)
@@ -158,8 +164,8 @@ def tile_multiheadlatentattention_pa_t_kernel(tc, x, w_dq, q_a_norm, w_uq, out):
             nc.scalar.copy(out=dst, in_=planes)
 
         def q_x(u):
-            xc = work.tile([P, UNIT * 2 * P], U32, align_bytes=64, name="xc", bufs=5)
-            xs = work.tile([P, UNIT * 2 * P], U8, align_bytes=64, name="xs", bufs=5)
+            xc = work.tile([P, UNIT * 2 * P], U32, align_bytes=64, name="xc", bufs=4)
+            xs = work.tile([P, UNIT * 2 * P], U8, align_bytes=64, name="xs", bufs=4)
             nc.vector.quantize_mx(out=xc[:].bitcast(FP8X4), scales=xs[:],
                                   in_=st["xg", u][:].rearrange("p i g w t -> p (i g w t)"))
             st["xc", u] = (xc, xs)
@@ -217,7 +223,7 @@ def tile_multiheadlatentattention_pa_t_kernel(tc, x, w_dq, q_a_norm, w_uq, out):
 
         def mx2(u):
             hc, hs = st["hc", u]
-            if u == UNITS - 1:
+            if u >= UNITS - LAG_M2 and (UNITS - 1 - u) % 2 == 0:
                 q_ps = psum.tile([P, 4, P], F32, name="xt", bufs=2)[:].rearrange("p (i r) w -> p i (r w)", i=UNIT)
             else:
                 q_ps = psum.tile([P, UNIT, NOUT], F32, name="q_ps", bufs=1)
@@ -230,7 +236,7 @@ def tile_multiheadlatentattention_pa_t_kernel(tc, x, w_dq, q_a_norm, w_uq, out):
         def rope(u):
             q_ps = st["q", u]
             b, t0 = u // UPB, (u % UPB) * UNIT
-            o_sb = work.tile([P, UNIT, H, QK], F32, name="o_sb", bufs=4)
+            o_sb = work.tile([P, UNIT, H, QK], F32, name="o_sb", bufs=UNITS)
             prod = work.tile([P, UNIT, 2, H, ROPE], F32, name="prod", bufs=UNITS)
             nc.vector.tensor_tensor(
                 out=prod[:],
@@ -240,7 +246,7 @@ def tile_multiheadlatentattention_pa_t_kernel(tc, x, w_dq, q_a_norm, w_uq, out):
                 op=ALU.mult)
             nc.vector.tensor_copy(out=o_sb[:, :, :, 0:NOPE],
                                   in_=q_ps[:, :, 0:H * NOPE].rearrange("p i (h f) -> p i h f", h=H))
-            adder = nc.vector if u == UNITS - 1 else nc.gpsimd
+            adder = nc.vector if u >= UNITS - 2 else nc.gpsimd
             for r in range(2):
                 adder.tensor_tensor(out=o_sb[:, :, :, NOPE + r * HALF:NOPE + (r + 1) * HALF],
                                     in0=prod[:, :, 0, :, r * HALF:(r + 1) * HALF],
@@ -252,8 +258,8 @@ def tile_multiheadlatentattention_pa_t_kernel(tc, x, w_dq, q_a_norm, w_uq, out):
             nc.tensor.matmul(st["g"][:], lhsT=ones[:], rhs=g_row[:], start=True, stop=True)
 
         def gain_copy():
-            nc.scalar.copy(out=g_b[:].rearrange("p (u m e) -> p u m e", u=2, e=2),
-                           in_=st["g"][:].rearrange("p (m u e) -> p u m e", u=2, e=2))
+            nc.vector.tensor_copy(out=g_b[:].rearrange("p (u m e) -> p u m e", u=2, e=2),
+                                  in_=st["g"][:].rearrange("p (m u e) -> p u m e", u=2, e=2))
 
         def on(fn, u, *which):
             if 0 <= u < UNITS:
@@ -263,10 +269,13 @@ def tile_multiheadlatentattention_pa_t_kernel(tc, x, w_dq, q_a_norm, w_uq, out):
             on(rope, s - LAG_ROPE)
             on(q_x, s - LAG_QX)
             if s == 1:
+                sine()
+                gain_spread()
                 weights_quantise(0)
                 weights_copy(1, 0, nc.vector.tensor_copy)
                 weights_copy(1, 1, nc.vector.tensor_copy)
                 weights_quantise(1)
+                gain_copy()
             on(t_x, s, 0)
             on(t_x, s, 1)
             on(t_h, s - LAG_TH, 0)
@@ -280,18 +289,18 @@ def tile_multiheadlatentattention_pa_t_kernel(tc, x, w_dq, q_a_norm, w_uq, out):
             on(c_x, s, 1)
             on(c_h, s - LAG_TH)
             if s == 0:
-                gain_spread()
                 weights_copy(0, 0, nc.vector.tensor_copy)
                 weights_copy(0, 1, nc.scalar.copy)
                 sine_half()
             if s == 1:
-                gain_copy()
-                tables()
+                root_table()
             if s == 2:
+                tables()
+            if s == 3:
                 weights_up()
             on(s_q, s - LAG_M1, 0)
             on(s_q, s - LAG_M1, 1)
-            if s == 3:
-                weights_up_quantise()
             on(q_h, s - LAG_TH)
+            if s == 4:
+                weights_up_quantise()
             on(load, s + AHEAD)

@@ -61,11 +61,17 @@ def tile_multiheadlatentattention_pa_t_kernel(tc, x, w_dq, q_a_norm, w_uq, out):
 
         w_raw = setup.tile([P, 2, 4 * Q_RANK], BF16)
         w_view = w_dq.rearrange("(g p t) c -> p g (t c)", g=2, p=P, t=4)
+        pos_i = setup.tile([P, TPB], I32)
+        nc.gpsimd.iota(pos_i[:], pattern=[[1, TPB]], base=0, channel_multiplier=TPB)
+        zero = setup.tile([P, 1], F32)
+        nc.vector.memset(zero[:], 0.0)
+        one = setup.tile([P, 1], F32)
+        nc.vector.memset(one[:], 1.0)
         g_row = setup.tile([P, Q_RANK], BF16)
-        nc.gpsimd.memset(g_row[:], 0.0)
+        nc.vector.memset(g_row[:], 0.0)
         load(0)
-        nc.sync.dma_start(out=g_row[0:1, :], in_=q_a_norm.rearrange("(o c) -> o c", o=1))
         nc.sync.dma_start(out=w_raw[:, 0, :], in_=w_view[:, 0, :])
+        nc.sync.dma_start(out=g_row[0:1, :], in_=q_a_norm.rearrange("(o c) -> o c", o=1))
         load(1)
         nc.sync.dma_start(out=w_raw[:, 1, :], in_=w_view[:, 1, :])
         load(2)
@@ -74,47 +80,43 @@ def tile_multiheadlatentattention_pa_t_kernel(tc, x, w_dq, q_a_norm, w_uq, out):
         for u in range(3, AHEAD):
             load(u)
 
-        pos_i = setup.tile([P, TPB], I32)
-        nc.gpsimd.iota(pos_i[:], pattern=[[1, TPB]], base=0, channel_multiplier=TPB)
         ident_f = const.tile([P, P], F32)
         make_identity(nc, ident_f[:])
         g_b = const.tile([P, Q_RANK], BF16)
         ones = setup.tile([P, P], BF16)
         nc.gpsimd.memset(ones[:], 1.0)
 
-        zero = setup.tile([P, 1], F32)
-        nc.vector.memset(zero[:], 0.0)
         warm = setup.tile([P, 1], F32)
         nc.scalar.activation(out=warm[:], in_=zero[:], func=ACT.Sin)
+        freq = setup.tile([P, HALF], F32)
+        for i in range(8):
+            nc.vector.tensor_scalar(out=freq[:, i:i + 1], in0=one[:], scalar1=1.0 / THETA ** (i / HALF) / (2.0 * math.pi),
+                                    scalar2=None, op0=ALU.mult)
+        for k in range(1, HALF // 8):
+            nc.vector.tensor_scalar(out=freq[:, 8 * k:8 * (k + 1)], in0=freq[:, 0:8], scalar1=THETA ** (-8.0 * k / HALF),
+                                    scalar2=None, op0=ALU.mult)
         pos_f = setup.tile([P, TPB], F32)
         nc.vector.tensor_copy(out=pos_f[:], in_=pos_i[:])
-        turns = setup.tile([P, HALF, TPB], F32)
-        for i in range(HALF):
-            freq = 1.0 / THETA ** (i / HALF) / (2.0 * math.pi)
-            if i < HALF // 2:
-                nc.vector.tensor_scalar(out=turns[:, i, :], in0=pos_f[:], scalar1=freq, scalar2=None, op0=ALU.mult)
-            else:
-                nc.scalar.activation(out=turns[:, i, :], in_=pos_f[:], func=ACT.Copy, scale=freq)
-        whole = setup.tile([P, HALF, TPB], I32)
+        turns = setup.tile([P, TPB, HALF], F32)
+        nc.vector.tensor_tensor(out=turns[:], in0=pos_f[:].unsqueeze(2).to_broadcast([P, TPB, HALF]),
+                                in1=freq[:].unsqueeze(1).to_broadcast([P, TPB, HALF]), op=ALU.mult)
+        whole = setup.tile([P, TPB, HALF], I32)
         part = setup.tile([P, TPB, HALF], F32)
         half = setup.tile([P, TPB, HALF], F32)
         trig = const.tile([P, TPB, 2, ROPE], F32)
 
         nc.vector.tensor_copy(out=whole[:], in_=turns[:])
-        nc.vector.tensor_tensor(out=part[:], in0=turns[:].rearrange("p i t -> p t i"),
-                                in1=whole[:].rearrange("p i t -> p t i"), op=ALU.subtract)
+        nc.vector.tensor_tensor(out=part[:], in0=turns[:], in1=whole[:], op=ALU.subtract)
 
-        def sine_half():
+        def sines():
             nc.scalar.activation(out=half[:], in_=part[:], func=ACT.Sin, scale=math.pi)
-
-        def sine():
             nc.scalar.activation(out=trig[:, :, 1, 0:HALF], in_=part[:], func=ACT.Sin, scale=2.0 * math.pi)
 
         def root_table():
             nc.scalar.activation(out=warm[:], in_=zero[:], func=ACT.Abs_reciprocal_sqrt, bias=1.0)
 
         def tables():
-            nc.gpsimd.tensor_tensor(out=half[:], in0=half[:], in1=half[:], op=ALU.mult)
+            nc.vector.tensor_tensor(out=half[:], in0=half[:], in1=half[:], op=ALU.mult)
             for r in range(2):
                 nc.gpsimd.tensor_scalar(out=trig[:, :, 0, r * HALF:(r + 1) * HALF], in0=half[:],
                                         scalar1=-2.0, scalar2=1.0, op0=ALU.mult, op1=ALU.add)
@@ -267,17 +269,18 @@ def tile_multiheadlatentattention_pa_t_kernel(tc, x, w_dq, q_a_norm, w_uq, out):
 
         for s in range(UNITS + LAG_ROPE):
             on(rope, s - LAG_ROPE)
+            if s == 1:
+                weights_quantise(0)
             on(q_x, s - LAG_QX)
             if s == 1:
-                sine()
-                gain_spread()
-                weights_quantise(0)
                 weights_copy(1, 0, nc.vector.tensor_copy)
                 weights_copy(1, 1, nc.vector.tensor_copy)
                 weights_quantise(1)
-                gain_copy()
             on(t_x, s, 0)
             on(t_x, s, 1)
+            if s == 1:
+                gain_spread()
+                gain_copy()
             on(t_h, s - LAG_TH, 0)
             on(t_h, s - LAG_TH, 1)
             on(mx1, s - LAG_M1, 0)
@@ -285,17 +288,17 @@ def tile_multiheadlatentattention_pa_t_kernel(tc, x, w_dq, q_a_norm, w_uq, out):
             on(mx2, s - LAG_M2)
             on(c_x, s, 0)
             on(r_t, s - LAG_NORM)
+            if s == LAG_NORM:
+                tables()
             on(norm, s - LAG_NORM)
             on(c_x, s, 1)
             on(c_h, s - LAG_TH)
             if s == 0:
                 weights_copy(0, 0, nc.vector.tensor_copy)
-                weights_copy(0, 1, nc.scalar.copy)
-                sine_half()
+                weights_copy(0, 1, nc.vector.tensor_copy)
+                sines()
             if s == 1:
                 root_table()
-            if s == 2:
-                tables()
             if s == 3:
                 weights_up()
             on(s_q, s - LAG_M1, 0)

from contextlib import ExitStack
import math

import concourse.mybir as mybir
from concourse.masks import make_identity

F32 = mybir.dt.float32
BF16 = mybir.dt.bfloat16
I32 = mybir.dt.int32
U32 = mybir.dt.uint32
U8 = mybir.dt.uint8
FP8X4 = mybir.dt.float8_e4m3fn_x4
ALU = mybir.AluOpType
ACT = mybir.ActivationFunctionType

P = 128
B, S, D, H, NOPE, ROPE, Q_RANK = 4, 2048, 1024, 2, 64, 64, 512
QK = NOPE + ROPE
HALF = ROPE // 2
NOUT = H * QK
EPS = 1e-6
THETA = 10000.0
TPB = S // P
UNIT = 2
UPB = TPB // UNIT
UNITS = B * UPB
AHEAD = 4
LAG_QX, LAG_M1, LAG_NORM, LAG_TH, LAG_M2, LAG_ROPE = 1, 2, 3, 4, 5, 6

FLOPS = 2 * B * S * (D * Q_RANK + Q_RANK * NOUT)


def tile_multiheadlatentattention_pa_t_kernel(tc, x, w_dq, q_a_norm, w_uq, out):
    nc = tc.nc
    xv = x.rearrange("b (p t) k -> b p t k", t=TPB)
    ov = out.rearrange("b (p t) h f -> b p t (h f)", t=TPB)

    with ExitStack() as ctx:
        const = ctx.enter_context(tc.tile_pool(name="const", bufs=1))
        setup = ctx.enter_context(tc.tile_pool(name="setup", bufs=1))
        xpool = ctx.enter_context(tc.tile_pool(name="xpool", bufs=AHEAD // 2 + 1))
        work = ctx.enter_context(tc.tile_pool(name="work", bufs=3))
        small = ctx.enter_context(tc.tile_pool(name="small", bufs=4))
        psum = ctx.enter_context(tc.psum_pool(name="psum", bufs=1))
        ctx.enter_context(tc.manual_schedule())
        st = {}

        def load(u):
            b, t0 = u // UPB, (u % UPB) * UNIT
            if u % 2 == 0:
                st["xx", u // 2] = xpool.tile([P, 2, UNIT, D], BF16, name="x_sb")
            x_sb = st["xx", u // 2]
            st["x", u] = x_sb[:, u % 2]
            if u < 2:
                for i in range(UNIT):
                    nc.sync.dma_start(out=x_sb[:, u, i, :], in_=xv[b, :, t0 + i, :])
            elif u < AHEAD:
                nc.sync.dma_start(out=x_sb[:, u % 2], in_=xv[b, :, t0:t0 + UNIT, :])
            elif u % 2 == 0:
                nc.sync.dma_start(out=x_sb[:].rearrange("p e i k -> p (e i) k"), in_=xv[b, :, t0:t0 + 2 * UNIT, :])

        w_raw = setup.tile([P, 2, 4 * Q_RANK], BF16)
        w_view = w_dq.rearrange("(g p t) c -> p g (t c)", g=2, p=P, t=4)
        pos_i = setup.tile([P, TPB], I32)
        nc.gpsimd.iota(pos_i[:], pattern=[[1, TPB]], base=0, channel_multiplier=TPB)
        zero = setup.tile([P, 1], F32)
        nc.vector.memset(zero[:], 0.0)
        one = setup.tile([P, 1], F32)
        nc.vector.memset(one[:], 1.0)
        g_row = setup.tile([P, Q_RANK], BF16)
        nc.vector.memset(g_row[:], 0.0)
        load(0)
        nc.sync.dma_start(out=w_raw[:, 0, :], in_=w_view[:, 0, :])
        nc.sync.dma_start(out=g_row[0:1, :], in_=q_a_norm.rearrange("(o c) -> o c", o=1))
        load(1)
        nc.sync.dma_start(out=w_raw[:, 1, :], in_=w_view[:, 1, :])
        load(2)
        u_raw = setup.tile([P, 4, NOUT], BF16)
        nc.sync.dma_start(out=u_raw[:], in_=w_uq.rearrange("(p j) n -> p j n", j=4))
        for u in range(3, AHEAD):
            load(u)

        ident_f = const.tile([P, P], F32)
        make_identity(nc, ident_f[:])
        g_b = const.tile([P, Q_RANK], BF16)
        ones = setup.tile([P, P], BF16)
        nc.gpsimd.memset(ones[:], 1.0)

        warm = setup.tile([P, 1], F32)
        nc.scalar.activation(out=warm[:], in_=zero[:], func=ACT.Sin)
        freq = setup.tile([P, HALF], F32)
        for i in range(8):
            nc.vector.tensor_scalar(out=freq[:, i:i + 1], in0=one[:], scalar1=1.0 / THETA ** (i / HALF) / (2.0 * math.pi),
                                    scalar2=None, op0=ALU.mult)
        for k in range(1, HALF // 8):
            nc.vector.tensor_scalar(out=freq[:, 8 * k:8 * (k + 1)], in0=freq[:, 0:8], scalar1=THETA ** (-8.0 * k / HALF),
                                    scalar2=None, op0=ALU.mult)
        pos_f = setup.tile([P, TPB], F32)
        nc.vector.tensor_copy(out=pos_f[:], in_=pos_i[:])
        turns = setup.tile([P, TPB, HALF], F32)
        nc.vector.tensor_tensor(out=turns[:], in0=pos_f[:].unsqueeze(2).to_broadcast([P, TPB, HALF]),
                                in1=freq[:].unsqueeze(1).to_broadcast([P, TPB, HALF]), op=ALU.mult)
        whole = setup.tile([P, TPB, HALF], I32)
        part = setup.tile([P, TPB, HALF], F32)
        half = setup.tile([P, TPB, HALF], F32)
        trig = const.tile([P, TPB, 2, ROPE], F32)

        nc.vector.tensor_copy(out=whole[:], in_=turns[:])
        nc.vector.tensor_tensor(out=part[:], in0=turns[:], in1=whole[:], op=ALU.subtract)

        def sines():
            nc.scalar.activation(out=half[:], in_=part[:], func=ACT.Sin, scale=math.pi)
            nc.scalar.activation(out=trig[:, :, 1, 0:HALF], in_=part[:], func=ACT.Sin, scale=2.0 * math.pi)

        def root_table():
            nc.scalar.activation(out=warm[:], in_=zero[:], func=ACT.Abs_reciprocal_sqrt, bias=1.0)

        def tables():
            nc.vector.tensor_tensor(out=half[:], in0=half[:], in1=half[:], op=ALU.mult)
            for r in range(2):
                nc.gpsimd.tensor_scalar(out=trig[:, :, 0, r * HALF:(r + 1) * HALF], in0=half[:],
                                        scalar1=-2.0, scalar2=1.0, op0=ALU.mult, op1=ALU.add)
            nc.gpsimd.tensor_scalar(out=trig[:, :, 1, HALF:], in0=trig[:, :, 1, 0:HALF],
                                    scalar1=-1.0, scalar2=0.0, op0=ALU.mult, op1=ALU.add)

        wdq_c = const.tile([P, 2, Q_RANK], U32, align_bytes=64)
        wdq_s = const.tile([P, 2, Q_RANK], U8, align_bytes=64)
        w_grps = []

        def weights_copy(g, u, copy):
            if u == 0:
                w_grps.append(setup.tile([P, Q_RANK, 4], BF16, align_bytes=64, name="w_grp%d" % g))
            copy(out=w_grps[g][:, 2 * P * u:2 * P * (u + 1), :].rearrange("p (m e) t -> p m e t", e=2),
                 in_=w_raw[:, g, :].rearrange("p (t m u e) -> p u m e t", t=4, u=2, e=2)[:, u])

        def weights_quantise(g):
            nc.vector.quantize_mx(out=wdq_c[:, g, :].bitcast(FP8X4), scales=wdq_s[:, g, :],
                                  in_=w_grps[g][:].rearrange("p c t -> p (c t)"))

        wuq_c = const.tile([P, NOUT], U32, align_bytes=64)
        wuq_s = const.tile([P, NOUT], U8, align_bytes=64)
        u_grp = setup.tile([P, 2, H, NOPE, 4], BF16, align_bytes=64)

        def weights_up():
            u_src = u_raw[:].rearrange("p j (h r f) -> p r h f j", h=H, r=2)
            for r in range(2):
                nc.vector.tensor_copy(out=u_grp[:, r], in_=u_src[:, r])

        def weights_up_quantise():
            nc.vector.quantize_mx(out=wuq_c[:].bitcast(FP8X4), scales=wuq_s[:],
                                  in_=u_grp[:].rearrange("p r h f j -> p (r h f j)"))

        def t_x(u, i):
            if i == 0:
                st["xg", u] = work.tile([P, UNIT, 2, P, 4], BF16, align_bytes=64, name="xg")
            xt = psum.tile([P, 4, P], F32, name="xt", bufs=2)
            words = st["x", u][:, i, :].bitcast(F32)
            for a in range(4):
                first = 2 * P * (a // 2) + a % 2
                nc.tensor.transpose(xt[:, a, :], words[:, first:first + 2 * P - 1:2], ident_f[:])
            st["xt", u, i] = xt

        def c_x(u, i):
            planes = st["xt", u, i][:].rearrange("p (g u) w -> p g w u", u=2)
            dst = st["xg", u][:, i].bitcast(F32)
            nc.scalar.copy(out=dst, in_=planes)

        def q_x(u):
            xc = work.tile([P, UNIT * 2 * P], U32, align_bytes=64, name="xc", bufs=4)
            xs = work.tile([P, UNIT * 2 * P], U8, align_bytes=64, name="xs", bufs=4)
            nc.vector.quantize_mx(out=xc[:].bitcast(FP8X4), scales=xs[:],
                                  in_=st["xg", u][:].rearrange("p i g w t -> p (i g w t)"))
            st["xc", u] = (xc, xs)

        def mx1(u, i):
            xc, xs = st["xc", u]
            c_ps = psum.tile([P, Q_RANK], F32, name="c_ps", bufs=4)
            for g in range(2):
                cols = slice((2 * i + g) * P, (2 * i + g + 1) * P)
                nc.tensor.matmul_mx(out=c_ps[:], lhsT=xc[:, cols].bitcast(FP8X4), lhsT_scale=xs[:, cols],
                                    rhs=wdq_c[:, g, :].bitcast(FP8X4), rhs_scale=wdq_s[:, g, :],
                                    start=(g == 0), stop=(g == 1))
            st["c", u, i] = c_ps

        def s_q(u, i):
            if i == 0:
                st["ss", u] = small.tile([P, UNIT], F32, name="ss")
            junk = work.tile([P, Q_RANK], BF16, name="junk")
            nc.scalar.activation(out=junk[:], in_=st["c", u, i][:], func=ACT.Square,
                                 accum_out=st["ss", u][:, i:i + 1])

        def r_t(u):
            rstd = small.tile([P, UNIT], F32, name="rstd")
            nc.scalar.activation(out=rstd[:], in_=st["ss", u][:], func=ACT.Abs_reciprocal_sqrt, scale=1.0 / Q_RANK,
                                 bias=EPS)
            st["rstd", u] = rstd

        def norm(u):
            rstd = st["rstd", u]
            h_sb = work.tile([P, UNIT, Q_RANK], BF16, name="h_sb")
            for i in range(UNIT):
                nc.vector.scalar_tensor_tensor(out=h_sb[:, i, :], in0=st["c", u, i][:], scalar=rstd[:, i:i + 1],
                                               in1=g_b[:], op0=ALU.mult, op1=ALU.mult)
            st["h", u] = h_sb

        def t_h(u, i):
            if i == 0:
                st["ht", u] = psum.tile([P, UNIT, 2, P], F32, name="ht", bufs=1)
            words = st["h", u][:, i, :].bitcast(F32)
            for j in range(2):
                nc.tensor.transpose(st["ht", u][:, i, j, :], words[:, j * P:(j + 1) * P], ident_f[:])

        def c_h(u):
            hg = work.tile([P, UNIT, P, 4], BF16, align_bytes=64, name="hg")
            nc.scalar.copy(out=hg[:].rearrange("p i w j -> p i (w j)").bitcast(F32).rearrange("p i (w j) -> p i w j", j=2),
                           in_=st["ht", u][:].rearrange("p i j w -> p i w j"))
            st["hg", u] = hg

        def q_h(u):
            hc = work.tile([P, UNIT * P], U32, align_bytes=64, name="hc")
            hs = work.tile([P, UNIT * P], U8, align_bytes=64, name="hs")
            nc.vector.quantize_mx(out=hc[:].bitcast(FP8X4), scales=hs[:],
                                  in_=st["hg", u][:].rearrange("p i w j -> p (i w j)"))
            st["hc", u] = (hc, hs)

        def mx2(u):
            hc, hs = st["hc", u]
            if u >= UNITS - LAG_M2 and (UNITS - 1 - u) % 2 == 0:
                q_ps = psum.tile([P, 4, P], F32, name="xt", bufs=2)[:].rearrange("p (i r) w -> p i (r w)", i=UNIT)
            else:
                q_ps = psum.tile([P, UNIT, NOUT], F32, name="q_ps", bufs=1)
            for i in range(UNIT):
                cols = slice(i * P, (i + 1) * P)
                nc.tensor.matmul_mx(out=q_ps[:, i, :], lhsT=hc[:, cols].bitcast(FP8X4), lhsT_scale=hs[:, cols],
                                    rhs=wuq_c[:].bitcast(FP8X4), rhs_scale=wuq_s[:], start=True, stop=True)
            st["q", u] = q_ps

        def rope(u):
            q_ps = st["q", u]
            b, t0 = u // UPB, (u % UPB) * UNIT
            o_sb = work.tile([P, UNIT, H, QK], F32, name="o_sb", bufs=UNITS)
            prod = work.tile([P, UNIT, 2, H, ROPE], F32, name="prod", bufs=UNITS)
            nc.vector.tensor_tensor(
                out=prod[:],
                in0=q_ps[:, :, H * NOPE:].rearrange("p i (h f) -> p i h f", h=H).unsqueeze(2).to_broadcast(
                    [P, UNIT, 2, H, ROPE]),
                in1=trig[:, t0:t0 + UNIT].unsqueeze(3).to_broadcast([P, UNIT, 2, H, ROPE]),
                op=ALU.mult)
            nc.vector.tensor_copy(out=o_sb[:, :, :, 0:NOPE],
                                  in_=q_ps[:, :, 0:H * NOPE].rearrange("p i (h f) -> p i h f", h=H))
            adder = nc.vector if u >= UNITS - 2 else nc.gpsimd
            for r in range(2):
                adder.tensor_tensor(out=o_sb[:, :, :, NOPE + r * HALF:NOPE + (r + 1) * HALF],
                                    in0=prod[:, :, 0, :, r * HALF:(r + 1) * HALF],
                                    in1=prod[:, :, 1, :, (1 - r) * HALF:(2 - r) * HALF], op=ALU.add)
            nc.sync.dma_start(out=ov[b, :, t0:t0 + UNIT, :], in_=o_sb[:].rearrange("p i h f -> p i (h f)"))

        def gain_spread():
            st["g"] = psum.tile([P, Q_RANK], F32, name="c_ps", bufs=4)
            nc.tensor.matmul(st["g"][:], lhsT=ones[:], rhs=g_row[:], start=True, stop=True)

        def gain_copy():
            nc.vector.tensor_copy(out=g_b[:].rearrange("p (u m e) -> p u m e", u=2, e=2),
                                  in_=st["g"][:].rearrange("p (m u e) -> p u m e", u=2, e=2))

        def on(fn, u, *which):
            if 0 <= u < UNITS:
                fn(u, *which)

        for s in range(UNITS + LAG_ROPE):
            on(rope, s - LAG_ROPE)
            if s == 1:
                weights_quantise(0)
            on(q_x, s - LAG_QX)
            if s == 1:
                weights_copy(1, 0, nc.vector.tensor_copy)
                weights_copy(1, 1, nc.vector.tensor_copy)
                weights_quantise(1)
            on(t_x, s, 0)
            on(t_x, s, 1)
            if s == 1:
                gain_spread()
                gain_copy()
            on(t_h, s - LAG_TH, 0)
            on(t_h, s - LAG_TH, 1)
            on(mx1, s - LAG_M1, 0)
            on(mx1, s - LAG_M1, 1)
            on(mx2, s - LAG_M2)
            on(c_x, s, 0)
            on(r_t, s - LAG_NORM)
            if s == LAG_NORM:
                tables()
            on(norm, s - LAG_NORM)
            on(c_x, s, 1)
            on(c_h, s - LAG_TH)
            if s == 0:
                weights_copy(0, 0, nc.vector.tensor_copy)
                weights_copy(0, 1, nc.vector.tensor_copy)
                sines()
            if s == 1:
                root_table()
            if s == 3:
                weights_up()
            on(s_q, s - LAG_M1, 0)
            on(s_q, s - LAG_M1, 1)
            on(q_h, s - LAG_TH)
            if s == 4:
                weights_up_quantise()
            on(load, s + AHEAD)
